import numpy as np
import ml_dtypes

BF16 = ml_dtypes.bfloat16


def bf(x):
    return np.asarray(x, np.float32).astype(BF16)


def f32(x):
    return np.asarray(x, np.float32)


def f64(x):
    return np.asarray(x).astype(np.float64)


def striped(idx):
    return np.tile(idx.reshape(-1, 16).T, (8, 1))


V, D, M, N = 2048, 128, 128, 1024
SLOPE = 0.01


def leaky(v):
    return np.maximum(v, SLOPE * v)


def setup_inputs():
    return {"table": bf(np.random.standard_normal((D, V))), "w": bf(np.random.standard_normal((D, M)) / np.sqrt(D)), "b": f32(0.2 * np.random.standard_normal((M, 1))), "offs": striped(np.random.permutation(np.tile(np.arange(V), 2))[:N])}


def reference(table, w, b, offs):
    idx = offs[:16].T.reshape(-1)
    return leaky(f64(w).T @ f64(table)[:, idx] + f64(b))

@@ -1,0 +1,37 @@
+import concourse.mybir as mybir
+
+BF16, F32, U16 = mybir.dt.bfloat16, mybir.dt.float32, mybir.dt.uint16
+IDENTITY = mybir.ActivationFunctionType.Identity
+MULT, MAX = mybir.AluOpType.mult, mybir.AluOpType.max
+
+D, V, M, N = 128, 2048, 128, 1024
+SLOPE = 0.01
+PIECE = 512
+FLOPS = 2 * D * M * N
+
+
+def tile_wordbyword_kernel(tc, table, w, b, offs, out):
+    nc = tc.nc
+    with (
+        tc.tile_pool(name="held", bufs=1) as held,
+        tc.tile_pool(name="work", bufs=2) as work,
+        tc.psum_pool(name="psum", bufs=2) as psum,
+    ):
+        offsets = held.tile([128, N // 16], U16, name="offsets")
+        nc.sync.dma_start(offsets[:], offs)
+        words = held.tile([D, V], BF16, name="words")
+        nc.scalar.dma_start(words[:], table)
+        weights = held.tile([D, M], BF16, name="weights")
+        nc.gpsimd.dma_start(weights[:], w)
+        bias = held.tile([M, 1], F32, name="bias")
+        nc.gpsimd.dma_start(bias[:], b)
+
+        for p in range(N // PIECE):
+            piece_offsets = offsets[:, p * (PIECE // 16) : (p + 1) * (PIECE // 16)]
+            projected = psum.tile([M, PIECE], F32, name="projected")
+            nc.tensor.matmul(projected[:], weights[:], words[:].indirect(piece_offsets), start=True, stop=True)
+            biased = work.tile([M, PIECE], F32, name="biased")
+            nc.scalar.activation(biased[:], projected[:], IDENTITY, bias=bias[:], scale=1.0)
+            result = work.tile([M, PIECE], F32, name="result")
+            nc.vector.scalar_tensor_tensor(result[:], biased[:], SLOPE, biased[:], op0=MULT, op1=MAX)
+            nc.sync.dma_start(out[:, p * PIECE : (p + 1) * PIECE], result[:])

@@ -22,9 +22,9 @@ def tile_wordbyword_kernel(tc, table, w, b, offs, out):
         words = held.tile([D, V], BF16, name="words")
         nc.scalar.dma_start(words[:], table)
         weights = held.tile([D, M], BF16, name="weights")
-        nc.gpsimd.dma_start(weights[:], w)
+        nc.sync.dma_start(weights[:], w)
         bias = held.tile([M, 1], F32, name="bias")
-        nc.gpsimd.dma_start(bias[:], b)
+        nc.sync.dma_start(bias[:], b)
 
         for p in range(N // PIECE):
             piece_offsets = offsets[:, p * (PIECE // 16) : (p + 1) * (PIECE // 16)]

@@ -26,6 +26,10 @@ def tile_wordbyword_kernel(tc, table, w, b, offs, out):
         bias = held.tile([M, 1], F32, name="bias")
         nc.sync.dma_start(bias[:], b)
 
+        scratch = held.tile([M, 1], F32, name="scratch")
+        nc.vector.memset(scratch[:], 0.0)
+        nc.scalar.activation(scratch[:], scratch[:], IDENTITY)
+
         for p in range(N // PIECE):
             piece_offsets = offsets[:, p * (PIECE // 16) : (p + 1) * (PIECE // 16)]
             projected = psum.tile([M, PIECE], F32, name="projected")

@@ -6,7 +6,7 @@ MULT, MAX = mybir.AluOpType.mult, mybir.AluOpType.max
 
 D, V, M, N = 128, 2048, 128, 1024
 SLOPE = 0.01
-PIECE = 512
+PIECE = 256
 FLOPS = 2 * D * M * N
 
 
@@ -14,8 +14,8 @@ def tile_wordbyword_kernel(tc, table, w, b, offs, out):
     nc = tc.nc
     with (
         tc.tile_pool(name="held", bufs=1) as held,
-        tc.tile_pool(name="work", bufs=2) as work,
-        tc.psum_pool(name="psum", bufs=2) as psum,
+        tc.tile_pool(name="work", bufs=N // PIECE) as work,
+        tc.psum_pool(name="psum", bufs=N // PIECE) as psum,
     ):
         offsets = held.tile([128, N // 16], U16, name="offsets")
         nc.sync.dma_start(offsets[:], offs)

@@ -7,6 +7,8 @@ MULT, MAX = mybir.AluOpType.mult, mybir.AluOpType.max
 D, V, M, N = 128, 2048, 128, 1024
 SLOPE = 0.01
 PIECE = 256
+BANK = 512
+WARM_UP = 6
 FLOPS = 2 * D * M * N
 
 
@@ -16,6 +18,7 @@ def tile_wordbyword_kernel(tc, table, w, b, offs, out):
         tc.tile_pool(name="held", bufs=1) as held,
         tc.tile_pool(name="work", bufs=N // PIECE) as work,
         tc.psum_pool(name="psum", bufs=N // PIECE) as psum,
+        tc.psum_pool(name="idle", bufs=1) as idle,
     ):
         offsets = held.tile([128, N // 16], U16, name="offsets")
         nc.sync.dma_start(offsets[:], offs)
@@ -26,9 +29,13 @@ def tile_wordbyword_kernel(tc, table, w, b, offs, out):
         bias = held.tile([M, 1], F32, name="bias")
         nc.sync.dma_start(bias[:], b)
 
+        zeros = held.tile([D, BANK], BF16, name="zeros")
+        nc.vector.memset(zeros[:], 0.0)
         scratch = held.tile([M, 1], F32, name="scratch")
-        nc.vector.memset(scratch[:], 0.0)
-        nc.scalar.activation(scratch[:], scratch[:], IDENTITY)
+        nc.scalar.activation(scratch[:], zeros[:, 0:1], IDENTITY)
+        unread = idle.tile([M, BANK], F32, name="unread")
+        for i in range(WARM_UP):
+            nc.tensor.matmul(unread[:], zeros[:, :M], zeros[:], start=True, stop=True)
 
         for p in range(N // PIECE):
             piece_offsets = offsets[:, p * (PIECE // 16) : (p + 1) * (PIECE // 16)]

@@ -7,8 +7,6 @@ MULT, MAX = mybir.AluOpType.mult, mybir.AluOpType.max
 D, V, M, N = 128, 2048, 128, 1024
 SLOPE = 0.01
 PIECE = 256
-BANK = 512
-WARM_UP = 6
 FLOPS = 2 * D * M * N
 
 
@@ -18,7 +16,7 @@ def tile_wordbyword_kernel(tc, table, w, b, offs, out):
         tc.tile_pool(name="held", bufs=1) as held,
         tc.tile_pool(name="work", bufs=N // PIECE) as work,
         tc.psum_pool(name="psum", bufs=N // PIECE) as psum,
-        tc.psum_pool(name="idle", bufs=1) as idle,
+        tc.psum_pool(name="turn", bufs=1) as turn,
     ):
         offsets = held.tile([128, N // 16], U16, name="offsets")
         nc.sync.dma_start(offsets[:], offs)
@@ -26,16 +24,19 @@ def tile_wordbyword_kernel(tc, table, w, b, offs, out):
         nc.scalar.dma_start(words[:], table)
         weights = held.tile([D, M], BF16, name="weights")
         nc.sync.dma_start(weights[:], w)
-        bias = held.tile([M, 1], F32, name="bias")
-        nc.sync.dma_start(bias[:], b)
+        bias_row = held.tile([1, M], F32, name="bias_row")
+        nc.sync.dma_start(bias_row[:], b.rearrange("m one -> one m"))
 
-        zeros = held.tile([D, BANK], BF16, name="zeros")
-        nc.vector.memset(zeros[:], 0.0)
         scratch = held.tile([M, 1], F32, name="scratch")
-        nc.scalar.activation(scratch[:], zeros[:, 0:1], IDENTITY)
-        unread = idle.tile([M, BANK], F32, name="unread")
-        for i in range(WARM_UP):
-            nc.tensor.matmul(unread[:], zeros[:, :M], zeros[:], start=True, stop=True)
+        nc.vector.memset(scratch[:], 0.0)
+        nc.scalar.activation(scratch[:], scratch[:], IDENTITY)
+
+        one = held.tile([1, 1], F32, name="one")
+        nc.vector.memset(one[:], 1.0)
+        bias_psum = turn.tile([M, 1], F32, name="bias_psum")
+        nc.tensor.matmul(bias_psum[:], bias_row[:], one[:], start=True, stop=True)
+        bias = held.tile([M, 1], F32, name="bias")
+        nc.vector.tensor_copy(bias[:], bias_psum[:])
 
         for p in range(N // PIECE):
             piece_offsets = offsets[:, p * (PIECE // 16) : (p + 1) * (PIECE // 16)]

@@ -16,7 +16,6 @@ def tile_wordbyword_kernel(tc, table, w, b, offs, out):
         tc.tile_pool(name="held", bufs=1) as held,
         tc.tile_pool(name="work", bufs=N // PIECE) as work,
         tc.psum_pool(name="psum", bufs=N // PIECE) as psum,
-        tc.psum_pool(name="turn", bufs=1) as turn,
     ):
         offsets = held.tile([128, N // 16], U16, name="offsets")
         nc.sync.dma_start(offsets[:], offs)
@@ -24,19 +23,12 @@ def tile_wordbyword_kernel(tc, table, w, b, offs, out):
         nc.scalar.dma_start(words[:], table)
         weights = held.tile([D, M], BF16, name="weights")
         nc.sync.dma_start(weights[:], w)
-        bias_row = held.tile([1, M], F32, name="bias_row")
-        nc.sync.dma_start(bias_row[:], b.rearrange("m one -> one m"))
+        bias = held.tile([M, 1], F32, name="bias")
+        nc.scalar.dma_start(bias[:], b)
 
         scratch = held.tile([M, 1], F32, name="scratch")
         nc.vector.memset(scratch[:], 0.0)
         nc.scalar.activation(scratch[:], scratch[:], IDENTITY)
-
-        one = held.tile([1, 1], F32, name="one")
-        nc.vector.memset(one[:], 1.0)
-        bias_psum = turn.tile([M, 1], F32, name="bias_psum")
-        nc.tensor.matmul(bias_psum[:], bias_row[:], one[:], start=True, stop=True)
-        bias = held.tile([M, 1], F32, name="bias")
-        nc.vector.tensor_copy(bias[:], bias_psum[:])
 
         for p in range(N // PIECE):
             piece_offsets = offsets[:, p * (PIECE // 16) : (p + 1) * (PIECE // 16)]

@@ -6,7 +6,8 @@ MULT, MAX = mybir.AluOpType.mult, mybir.AluOpType.max
 
 D, V, M, N = 128, 2048, 128, 1024
 SLOPE = 0.01
-PIECE = 256
+PIECE = 128
+STORE = 256
 FLOPS = 2 * D * M * N
 
 
@@ -30,12 +31,16 @@ def tile_wordbyword_kernel(tc, table, w, b, offs, out):
         nc.vector.memset(scratch[:], 0.0)
         nc.scalar.activation(scratch[:], scratch[:], IDENTITY)
 
-        for p in range(N // PIECE):
-            piece_offsets = offsets[:, p * (PIECE // 16) : (p + 1) * (PIECE // 16)]
-            projected = psum.tile([M, PIECE], F32, name="projected")
-            nc.tensor.matmul(projected[:], weights[:], words[:].indirect(piece_offsets), start=True, stop=True)
-            biased = work.tile([M, PIECE], F32, name="biased")
-            nc.scalar.activation(biased[:], projected[:], IDENTITY, bias=bias[:], scale=1.0)
-            result = work.tile([M, PIECE], F32, name="result")
-            nc.vector.scalar_tensor_tensor(result[:], biased[:], SLOPE, biased[:], op0=MULT, op1=MAX)
-            nc.sync.dma_start(out[:, p * PIECE : (p + 1) * PIECE], result[:])
+        for s in range(N // STORE):
+            result = work.tile([M, STORE], F32, name="result")
+            for h in range(STORE // PIECE):
+                first = s * STORE + h * PIECE
+                piece_offsets = offsets[:, first // 16 : (first + PIECE) // 16]
+                projected = psum.tile([M, PIECE], F32, name="projected")
+                nc.tensor.matmul(projected[:], weights[:], words[:].indirect(piece_offsets), start=True, stop=True)
+                biased = work.tile([M, PIECE], F32, name="biased")
+                nc.scalar.activation(biased[:], projected[:], IDENTITY, bias=bias[:], scale=1.0)
+                nc.vector.scalar_tensor_tensor(
+                    result[:, h * PIECE : (h + 1) * PIECE], biased[:], SLOPE, biased[:], op0=MULT, op1=MAX
+                )
+            nc.sync.dma_start(out[:, s * STORE : (s + 1) * STORE], result[:])

@@ -18,12 +18,12 @@ def tile_wordbyword_kernel(tc, table, w, b, offs, out):
         tc.tile_pool(name="work", bufs=N // PIECE) as work,
         tc.psum_pool(name="psum", bufs=N // PIECE) as psum,
     ):
+        words = held.tile([D, V], BF16, name="words")
+        nc.sync.dma_start(words[:], table)
         offsets = held.tile([128, N // 16], U16, name="offsets")
         nc.sync.dma_start(offsets[:], offs)
-        words = held.tile([D, V], BF16, name="words")
-        nc.scalar.dma_start(words[:], table)
         weights = held.tile([D, M], BF16, name="weights")
-        nc.sync.dma_start(weights[:], w)
+        nc.scalar.dma_start(weights[:], w)
         bias = held.tile([M, 1], F32, name="bias")
         nc.scalar.dma_start(bias[:], b)
 

@@ -2,7 +2,7 @@ import concourse.mybir as mybir
 
 BF16, F32, U16 = mybir.dt.bfloat16, mybir.dt.float32, mybir.dt.uint16
 IDENTITY = mybir.ActivationFunctionType.Identity
-MULT, MAX = mybir.AluOpType.mult, mybir.AluOpType.max
+ADD, MULT, MAX = mybir.AluOpType.add, mybir.AluOpType.mult, mybir.AluOpType.max
 
 D, V, M, N = 128, 2048, 128, 1024
 SLOPE = 0.01
@@ -31,6 +31,9 @@ def tile_wordbyword_kernel(tc, table, w, b, offs, out):
         nc.vector.memset(scratch[:], 0.0)
         nc.scalar.activation(scratch[:], scratch[:], IDENTITY)
 
+        slope_bias = held.tile([M, 1], F32, name="slope_bias")
+        nc.vector.tensor_scalar_mul(slope_bias[:], bias[:], SLOPE)
+
         for s in range(N // STORE):
             result = work.tile([M, STORE], F32, name="result")
             for h in range(STORE // PIECE):
@@ -38,9 +41,9 @@ def tile_wordbyword_kernel(tc, table, w, b, offs, out):
                 piece_offsets = offsets[:, first // 16 : (first + PIECE) // 16]
                 projected = psum.tile([M, PIECE], F32, name="projected")
                 nc.tensor.matmul(projected[:], weights[:], words[:].indirect(piece_offsets), start=True, stop=True)
-                biased = work.tile([M, PIECE], F32, name="biased")
-                nc.scalar.activation(biased[:], projected[:], IDENTITY, bias=bias[:], scale=1.0)
+                sloped = work.tile([M, PIECE], F32, name="sloped")
+                nc.scalar.activation(sloped[:], projected[:], IDENTITY, bias=slope_bias[:], scale=SLOPE)
                 nc.vector.scalar_tensor_tensor(
-                    result[:, h * PIECE : (h + 1) * PIECE], biased[:], SLOPE, biased[:], op0=MULT, op1=MAX
+                    result[:, h * PIECE : (h + 1) * PIECE], projected[:], bias[:], sloped[:], op0=ADD, op1=MAX
                 )
             nc.sync.dma_start(out[:, s * STORE : (s + 1) * STORE], result[:])

@@ -42,7 +42,10 @@ def tile_wordbyword_kernel(tc, table, w, b, offs, out):
                 projected = psum.tile([M, PIECE], F32, name="projected")
                 nc.tensor.matmul(projected[:], weights[:], words[:].indirect(piece_offsets), start=True, stop=True)
                 sloped = work.tile([M, PIECE], F32, name="sloped")
-                nc.scalar.activation(sloped[:], projected[:], IDENTITY, bias=slope_bias[:], scale=SLOPE)
+                if first == 0:
+                    nc.vector.tensor_scalar(sloped[:], projected[:], SLOPE, slope_bias[:], op0=MULT, op1=ADD)
+                else:
+                    nc.scalar.activation(sloped[:], projected[:], IDENTITY, bias=slope_bias[:], scale=SLOPE)
                 nc.vector.scalar_tensor_tensor(
                     result[:, h * PIECE : (h + 1) * PIECE], projected[:], bias[:], sloped[:], op0=ADD, op1=MAX
                 )

import concourse.mybir as mybir

BF16, F32, U16 = mybir.dt.bfloat16, mybir.dt.float32, mybir.dt.uint16
IDENTITY = mybir.ActivationFunctionType.Identity
ADD, MULT, MAX = mybir.AluOpType.add, mybir.AluOpType.mult, mybir.AluOpType.max

D, V, M, N = 128, 2048, 128, 1024
SLOPE = 0.01
PIECE = 128
STORE = 256
FLOPS = 2 * D * M * N


def tile_wordbyword_kernel(tc, table, w, b, offs, out):
    nc = tc.nc
    with (
        tc.tile_pool(name="held", bufs=1) as held,
        tc.tile_pool(name="work", bufs=N // PIECE) as work,
        tc.psum_pool(name="psum", bufs=N // PIECE) as psum,
    ):
        words = held.tile([D, V], BF16, name="words")
        nc.sync.dma_start(words[:], table)
        offsets = held.tile([128, N // 16], U16, name="offsets")
        nc.sync.dma_start(offsets[:], offs)
        weights = held.tile([D, M], BF16, name="weights")
        nc.scalar.dma_start(weights[:], w)
        bias = held.tile([M, 1], F32, name="bias")
        nc.scalar.dma_start(bias[:], b)

        scratch = held.tile([M, 1], F32, name="scratch")
        nc.vector.memset(scratch[:], 0.0)
        nc.scalar.activation(scratch[:], scratch[:], IDENTITY)

        slope_bias = held.tile([M, 1], F32, name="slope_bias")
        nc.vector.tensor_scalar_mul(slope_bias[:], bias[:], SLOPE)

        for s in range(N // STORE):
            result = work.tile([M, STORE], F32, name="result")
            for h in range(STORE // PIECE):
                first = s * STORE + h * PIECE
                piece_offsets = offsets[:, first // 16 : (first + PIECE) // 16]
                projected = psum.tile([M, PIECE], F32, name="projected")
                nc.tensor.matmul(projected[:], weights[:], words[:].indirect(piece_offsets), start=True, stop=True)
                sloped = work.tile([M, PIECE], F32, name="sloped")
                if first == 0:
                    nc.vector.tensor_scalar(sloped[:], projected[:], SLOPE, slope_bias[:], op0=MULT, op1=ADD)
                else:
                    nc.scalar.activation(sloped[:], projected[:], IDENTITY, bias=slope_bias[:], scale=SLOPE)
                nc.vector.scalar_tensor_tensor(
                    result[:, h * PIECE : (h + 1) * PIECE], projected[:], bias[:], sloped[:], op0=ADD, op1=MAX
                )
            nc.sync.dma_start(out[:, s * STORE : (s + 1) * STORE], result[:])
